import numpy as np
import ml_dtypes


def mxq(x, axis, fmt="e4m3"):
    dtype, down = {"e4m3": (ml_dtypes.float8_e4m3fn, 7), "e5m2": (ml_dtypes.float8_e5m2, 14)}[fmt]
    v = np.moveaxis(np.asarray(x, np.float32).astype(ml_dtypes.bfloat16).astype(np.float64), axis, -1)
    blocks = v.reshape(v.shape[:-1] + (-1, 32))
    amax = np.abs(blocks).max(-1, keepdims=True)
    byte = np.maximum(np.where(amax > 0, np.frexp(amax)[1] - 1 + 127, 0) - down, 1)
    scale = np.exp2(byte - 127.0)
    codes = (blocks / scale).astype(np.float32).astype(dtype).astype(np.float64)
    return np.moveaxis((codes * scale).reshape(v.shape), -1, axis)


WIDE = False


def mx_kscale(k):
    if not WIDE:
        return np.ones(k)
    levels = np.array([10, -10, 5, -5, 0])
    if k % 512:
        return np.exp2(np.random.permutation(np.resize(levels, k // 32))).repeat(32)
    a = np.empty((k // 512, 16))
    for p in range(k // 512):
        a[p, :8] = np.random.permutation(np.resize(levels, 8))
        for g in range(8):
            far = levels[np.abs(levels - a[p, g]) >= 10]
            a[p, g + 8] = far[np.random.randint(len(far))]
    return np.exp2(a.ravel()).repeat(32)


BF16 = ml_dtypes.bfloat16


def bf(x):
    return np.asarray(x, np.float32).astype(BF16)


def f64(x):
    return np.asarray(x).astype(np.float64)


B, S, D, NH, LAT, F = 4, 128, 2048, 16, 512, 8192
EPS = 1e-5


def layer_norm(c, g, b):
    m = c.mean(-1, keepdims=True)
    v = ((c - m) ** 2).mean(-1, keepdims=True)
    return (c - m) * (1.0 / np.sqrt(v + EPS)) * g + b


def down_weight():
    return (np.random.standard_normal((D, LAT)) + 0.3 * np.random.standard_normal((D, 1))) / np.sqrt(D)


def draw0():
    s = mx_kscale(D)
    tq, tkv = mx_kscale(LAT), mx_kscale(LAT)
    return {
        "normed": bf(np.random.standard_normal((B, S, D)) * s),
        "W_dq": bf(down_weight() / s[:, None]),
        "q_ln_g": bf((1.0 + 0.1 * np.random.standard_normal(LAT)) * tq),
        "q_ln_b": bf(0.1 * np.random.standard_normal(LAT) * tq),
        "W_uq": bf(np.random.standard_normal((LAT, D)) / np.sqrt(LAT) / tq[:, None]),
        "W_dkv": bf(down_weight() / s[:, None]),
        "kv_ln_g": bf((1.0 + 0.1 * np.random.standard_normal(LAT)) * tkv),
        "kv_ln_b": bf(0.1 * np.random.standard_normal(LAT) * tkv),
        "W_ukv": bf(np.random.standard_normal((LAT, D + D)) / np.sqrt(LAT) / tkv[:, None]),
    }


def core(normed, W_dq, q_ln_g, q_ln_b, W_uq, W_dkv, kv_ln_g, kv_ln_b, W_ukv):
    nq = mxq(f64(normed), 2, "e4m3")
    cq = layer_norm(nq @ mxq(f64(W_dq), 0, "e4m3"), f64(q_ln_g), f64(q_ln_b))
    Q = mxq(cq, 2, "e4m3") @ mxq(f64(W_uq), 0, "e4m3")
    ckv = layer_norm(nq @ mxq(f64(W_dkv), 0, "e4m3"), f64(kv_ln_g), f64(kv_ln_b))
    KV = mxq(ckv, 2, "e4m3") @ mxq(f64(W_ukv), 0, "e4m3")
    return Q, KV


def e4m3fn_bytes(y):
    return np.clip(np.asarray(y, np.float64), -448.0, 448.0).astype(np.float32).astype(ml_dtypes.float8_e4m3fn).view(np.uint8)


def e4m3fn_values(b):
    return np.asarray(b, np.uint8).view(ml_dtypes.float8_e4m3fn).astype(np.float64)


def setup_inputs():
    d = draw0()
    x0 = np.asarray(d['W_ukv']).astype(np.float64)
    s = (np.max(np.abs(x0), axis=(1,), keepdims=True) / 448.0).astype(np.float32)
    out = {}
    for k, v in d.items():
        if k == 'W_ukv':
            out['W_ukv_bytes'] = e4m3fn_bytes(x0 / s.astype(np.float64))
            out['W_ukv_scale'] = s
        else:
            out[k] = v
    return out


def reference(normed, W_dq, q_ln_g, q_ln_b, W_uq, W_dkv, kv_ln_g, kv_ln_b, W_ukv_bytes, W_ukv_scale):
    return core(normed, W_dq, q_ln_g, q_ln_b, W_uq, W_dkv, kv_ln_g, kv_ln_b, e4m3fn_values(W_ukv_bytes) * W_ukv_scale.astype(np.float64))

from contextlib import ExitStack

import concourse.mybir as mybir
from concourse.masks import make_identity

F32 = mybir.dt.float32
BF16 = mybir.dt.bfloat16
U32 = mybir.dt.uint32
U8 = mybir.dt.uint8
F8 = mybir.dt.float8_e4m3fn
FP8X4 = mybir.dt.float8_e4m3fn_x4
ACT = mybir.ActivationFunctionType
ALU = mybir.AluOpType

P = 128
PACK = 4
TOK = 512
D = 2048
LAT = 512
NQ = 2048
NKV = 4096
EPS = 1e-5
TILES = TOK // P
PASSES = D // (P * PACK)
BANK = 512
CHUNK = 1024

FLOPS = 2 * TOK * D * LAT * 2 + 2 * TOK * LAT * (NQ + NKV)


def tile_transformerdecoderblock_pa_kernel(
    tc, normed, W_dq, q_ln_g, q_ln_b, W_uq, W_dkv, kv_ln_g, kv_ln_b, W_ukv_bytes, W_ukv_scale, out_q, out_kv
):
    nc = tc.nc
    with ExitStack() as ctx:
        keep = ctx.enter_context(tc.tile_pool(name="keep", bufs=1))
        work = ctx.enter_context(tc.tile_pool(name="work", bufs=3))
        psum = ctx.enter_context(tc.psum_pool(name="psum", bufs=2))

        x_rows = normed.rearrange("b s d -> (b s) d")
        x_raw = []
        wkv_raw = []
        wq_raw = []
        ub = []
        uq_raw = []

        def load_x(i):
            xr = work.tile([P, D], BF16, name="x_raw", tag="raw", bufs=9, align_bytes=64)
            nc.sync.dma_start(out=xr[:], in_=x_rows[i * P : (i + 1) * P, :])
            x_raw.append(xr)

        def load_down(src, g, dst, halves=1):
            wr = work.tile([P, PACK, LAT], BF16, name="w_raw", tag="raw", bufs=9, align_bytes=64)
            rows = src[g * BANK : (g + 1) * BANK, :].rearrange("(p j) n -> p j n", j=PACK)
            width = LAT // halves
            for h in range(halves):
                cols = slice(h * width, (h + 1) * width)
                nc.sync.dma_start(out=wr[:, :, cols], in_=rows[:, :, cols])
            dst.append(wr)

        def load_bytes(c):
            u = work.tile([P, PACK, CHUNK], U8, name="ukv_bytes", bufs=4, align_bytes=64)
            nc.sync.dma_start(
                out=u[:],
                in_=W_ukv_bytes.rearrange("(p j) n -> p j n", j=PACK)[:, :, c * CHUNK : (c + 1) * CHUNK],
            )
            ub.append(u)

        def load_uq(c):
            wr = work.tile([P, PACK, CHUNK], BF16, name="uq_raw", bufs=2, align_bytes=64)
            nc.sync.dma_start(
                out=wr[:], in_=W_uq.rearrange("(p j) n -> p j n", j=PACK)[:, :, c * CHUNK : (c + 1) * CHUNK]
            )
            uq_raw.append(wr)

        ident = keep.tile([P, P], F32, name="ident")
        make_identity(nc, ident[:])

        warm = keep.tile([P, 1], F32, name="warm")
        nc.gpsimd.memset(warm[:], 1.0)
        warm_out = keep.tile([P, 1], F32, name="warm_out")
        nc.scalar.activation(out=warm_out[:], in_=warm[:], func=ACT.Abs_reciprocal_sqrt)

        us = keep.tile([P, PACK], F32, name="us")
        nc.scalar.dma_start(out=us[:], in_=W_ukv_scale.rearrange("(p j) o -> p (j o)", j=PACK))

        def affine(vec, nm):
            raw = keep.tile([P, PACK], BF16, name=nm + "_raw")
            nc.scalar.dma_start(out=raw[:], in_=vec.rearrange("(p j) -> p j", j=PACK))
            full = keep.tile([P, PACK], F32, name=nm)
            nc.gpsimd.tensor_copy(out=full[:], in_=raw[:])
            return full

        g_kv = affine(kv_ln_g, "g_kv")
        b_kv = affine(kv_ln_b, "b_kv")
        g_q = affine(q_ln_g, "g_q")
        b_q = affine(q_ln_b, "b_q")

        load_down(W_dkv, 0, wkv_raw, halves=2)
        load_x(0)
        load_bytes(0)
        load_down(W_dkv, 1, wkv_raw)
        load_x(1)
        load_down(W_dkv, 2, wkv_raw)
        load_x(2)
        load_down(W_dkv, 3, wkv_raw)
        load_x(3)
        load_bytes(1)
        load_bytes(2)
        for g in range(PASSES):
            load_down(W_dq, g, wq_raw)
        load_bytes(3)
        load_uq(0)
        load_uq(1)

        x_codes = keep.tile([P, TILES, BANK], U32, name="x_codes", align_bytes=64)
        x_scales = keep.tile([P, TILES, BANK], U8, name="x_scales", align_bytes=64)
        wkv_codes = keep.tile([P, PASSES, LAT], U32, name="wkv_codes", align_bytes=64)
        wkv_scales = keep.tile([P, PASSES, LAT], U8, name="wkv_scales", align_bytes=64)
        wq_codes = keep.tile([P, PASSES, LAT], U32, name="wq_codes", align_bytes=64)
        wq_scales = keep.tile([P, PASSES, LAT], U8, name="wq_scales", align_bytes=64)
        uq_codes = keep.tile([P, NQ // BANK, BANK], U32, name="uq_codes", align_bytes=64)
        uq_scales = keep.tile([P, NQ // BANK, BANK], U8, name="uq_scales", align_bytes=64)
        ukv_codes = keep.tile([P, NKV // BANK, BANK], U32, name="ukv_codes", align_bytes=64)
        ukv_scales = keep.tile([P, NKV // BANK, BANK], U8, name="ukv_scales", align_bytes=64)

        def interleave(grouped, planes):
            nc.vector.tensor_copy(
                out=grouped.rearrange("p (c i j) -> p c j i", i=4, j=PACK),
                in_=planes.rearrange("p j (c i) -> p c j i", i=4),
            )

        def quantize(codes, scales, grouped):
            nc.vector.quantize_mx(out=codes.bitcast(FP8X4), scales=scales, in_=grouped)

        def prep_w(planes, codes, scales, halves=1):
            grp = work.tile([P, BANK * PACK], BF16, name="w_grp", bufs=4, align_bytes=64)
            width = BANK // halves
            for h in range(halves):
                interleave(
                    grp[:, h * width * PACK : (h + 1) * width * PACK], planes[:, :, h * width : (h + 1) * width]
                )
            quantize(codes, scales, grp[:])

        def prep_x(i):
            words = x_raw[i][:].bitcast(F32)
            grp = work.tile([P, D], BF16, name="x_grp", bufs=3, align_bytes=64)
            grp_words = grp[:].bitcast(F32)
            for h in range(2):
                xt = psum.tile([P, 2, 2, P], F32, name="tr", bufs=2)
                for gg in range(2):
                    g = 2 * h + gg
                    for u in range(2):
                        nc.tensor.transpose(
                            xt[:, gg, u, :], words[:, 256 * g + u : 256 * (g + 1) : 2], ident[:]
                        )
                nc.scalar.copy(
                    out=grp_words[:, h * 512 : (h + 1) * 512].rearrange("p (g r u) -> p g r u", g=2, u=2),
                    in_=xt[:].rearrange("p g u r -> p g r u"),
                )
            quantize(x_codes[:, i, :], x_scales[:, i, :], grp[:])

        def stage1(acc, i, g, codes, scales):
            nc.tensor.matmul_mx(
                out=acc[:],
                lhsT=x_codes[:, i, g * P : (g + 1) * P].bitcast(FP8X4),
                lhsT_scale=x_scales[:, i, g * P : (g + 1) * P],
                rhs=codes[:, g, :].bitcast(FP8X4),
                rhs_scale=scales[:, g, :],
                start=(g == 0),
                stop=(g == PASSES - 1),
            )

        def norm_pair(accs, g_col, b_col, label):
            mv = work.tile([P, 2, 2], F32, name="mv", bufs=2)
            for k in range(2):
                stats = work.tile([P, 6], F32, name="stats", bufs=4)
                nc.vector.bn_stats(out=stats[:], in_=accs[k][:])
                nc.vector.bn_aggr(out=mv[:, k, :], in_=stats[:])
            rstd = work.tile([P, 2], F32, name="rstd", bufs=2)
            nc.scalar.activation(out=rstd[:], in_=mv[:, :, 1], func=ACT.Abs_reciprocal_sqrt, bias=EPS)
            nm = work.tile([P, 2], F32, name="nm", bufs=2)
            nc.scalar.mul(nm[:], mv[:, :, 0], -1.0)
            halves = []
            for h in range(2):
                half = psum.tile([P, 2, 2 * P], F32, name="tr", bufs=2)
                halves.append(half)
            for k in range(2):
                nmr = work.tile([P, 1], F32, name="nmr", bufs=4)
                nc.scalar.activation(out=nmr[:], in_=nm[:, k : k + 1], func=ACT.Copy, scale=rstd[:, k : k + 1])
                y = work.tile([P, PACK, P], F32, name="y", bufs=3)
                nc.scalar.activation(
                    out=y[:],
                    in_=accs[k][:].rearrange("p (m t) -> p t m", t=PACK),
                    func=ACT.Identity,
                    scale=rstd[:, k : k + 1],
                    bias=nmr[:],
                )
                for t in range(PACK):
                    nc.tensor.transpose(halves[t // 2][:, t % 2, k * P : (k + 1) * P], y[:, t, :], ident[:])
            planes = work.tile([P, PACK, 2 * P], BF16, name="c_planes", bufs=2, align_bytes=64)
            for t in range(PACK):
                nc.scalar.activation(
                    out=planes[:, t, :],
                    in_=halves[t // 2][:, t % 2, :],
                    func=ACT.Identity,
                    scale=g_col[:, t : t + 1],
                    bias=b_col[:, t : t + 1],
                )
            grp = work.tile([P, 2 * P * PACK], BF16, name="c_grp", bufs=2, align_bytes=64)
            interleave(grp[:], planes[:])
            codes = keep.tile([P, 2 * P], U32, name="c_codes_" + label, align_bytes=64)
            scales = keep.tile([P, 2 * P], U8, name="c_scales_" + label, align_bytes=64)
            quantize(codes[:], scales[:], grp[:])
            return codes, scales

        def outputs(i, c, c_pairs, codes, scales, dst, engines):
            cc, cs = c_pairs[i // 2]
            cols = slice((i % 2) * P, (i % 2 + 1) * P)
            ob = work.tile([P, CHUNK], F32, name="ob", bufs=5)
            for h in range(2):
                n = 2 * c + h
                bank = psum.tile([P, BANK], F32, name="out_bank", bufs=3)
                nc.tensor.matmul_mx(
                    out=bank[:],
                    lhsT=cc[:, cols].bitcast(FP8X4),
                    lhsT_scale=cs[:, cols],
                    rhs=codes[:, n, :].bitcast(FP8X4),
                    rhs_scale=scales[:, n, :],
                    start=True,
                    stop=True,
                )
                if engines[h] == "S":
                    nc.scalar.copy(out=ob[:, h * BANK : (h + 1) * BANK], in_=bank[:])
                else:
                    nc.vector.tensor_copy(out=ob[:, h * BANK : (h + 1) * BANK], in_=bank[:])
            nc.sync.dma_start(out=dst[i * P : (i + 1) * P, c * CHUNK : (c + 1) * CHUNK], in_=ob[:])

        wide = {}

        def widen(c, engines):
            wide[c] = work.tile([P, PACK, CHUNK], BF16, name="ukv_wide", bufs=2, align_bytes=64)
            for t in range(PACK):
                src = ub[c][:, t, :].bitcast(F8)
                if engines[t] == "S":
                    nc.scalar.activation(out=wide[c][:, t, :], in_=src, func=ACT.Copy, scale=us[:, t : t + 1])
                else:
                    nc.vector.tensor_scalar(
                        out=wide[c][:, t, :], in0=src, scalar1=us[:, t : t + 1], scalar2=None, op0=ALU.mult
                    )

        def prep_ukv(c):
            grp = work.tile([P, CHUNK * PACK], BF16, name="u_grp", bufs=2, align_bytes=64)
            for h in range(2):
                half = PACK * BANK
                interleave(grp[:, h * half : (h + 1) * half], wide[c][:, :, h * BANK : (h + 1) * BANK])
            two = slice(2 * c, 2 * c + 2)
            quantize(
                ukv_codes[:, two, :].rearrange("p n w -> p (n w)"),
                ukv_scales[:, two, :].rearrange("p n w -> p (n w)"),
                grp[:],
            )

        def prep_uq(c):
            for h in range(2):
                n = 2 * c + h
                prep_w(uq_raw[c][:, :, h * BANK : (h + 1) * BANK], uq_codes[:, n, :], uq_scales[:, n, :])

        kv_rows = out_kv.rearrange("b s d -> (b s) d")
        q_rows = out_q.rearrange("b s d -> (b s) d")

        acc = {}
        for s in range(TILES):
            prep_w(wkv_raw[s][:], wkv_codes[:, s, :], wkv_scales[:, s, :], halves=2 if s == 0 else 1)
            prep_x(s)
            if s < 3:
                acc[s] = psum.tile([P, LAT], F32, name="acc", bufs=3)
                for g in range(s):
                    stage1(acc[s], s, g, wkv_codes, wkv_scales)
            for i in range(min(s + 1, 3)):
                stage1(acc[i], i, s, wkv_codes, wkv_scales)

        widen(0, "SSSS")
        kv_pairs = []
        kv_pairs.append(norm_pair((acc[0], acc[1]), g_kv, b_kv, "kv0"))
        acc[3] = psum.tile([P, LAT], F32, name="acc", bufs=3)
        for g in range(PASSES):
            stage1(acc[3], 3, g, wkv_codes, wkv_scales)
        kv_pairs.append(norm_pair((acc[2], acc[3]), g_kv, b_kv, "kv1"))

        def kv_out(c, e):
            for i in range(TILES):
                outputs(i, c, kv_pairs, ukv_codes, ukv_scales, kv_rows, e)

        prep_ukv(0)
        widen(1, "SSSS")
        kv_out(0, "SS")
        prep_ukv(1)
        widen(2, "SSSS")
        kv_out(1, "SS")
        for g in range(PASSES):
            prep_w(wq_raw[g][:], wq_codes[:, g, :], wq_scales[:, g, :])
        prep_ukv(2)
        widen(3, "SSSS")
        kv_out(2, "SS")
        q_pairs = []
        for k in range(2):
            accs = []
            for i in (2 * k, 2 * k + 1):
                a = psum.tile([P, LAT], F32, name="acc", bufs=3)
                for g in range(PASSES):
                    stage1(a, i, g, wq_codes, wq_scales)
                accs.append(a)
            q_pairs.append(norm_pair(accs, g_q, b_q, "q%d" % k))
        prep_ukv(3)
        kv_out(3, "SS")
        for c in range(NQ // CHUNK):
            prep_uq(c)
            for i in range(TILES):
                outputs(i, c, q_pairs, uq_codes, uq_scales, q_rows, "SV")
